import numpy as np
import ml_dtypes

BF16 = ml_dtypes.bfloat16


def bf(x):
    return np.asarray(x, np.float32).astype(BF16)


def f32(x):
    return np.asarray(x, np.float32)


def f64(x):
    return np.asarray(x).astype(np.float64)


def striped(idx):
    return np.tile(idx.reshape(-1, 16).T, (8, 1))


B, DESC, H, K, S, N = 3, 128, 128, 3, 2048, 1024
P = DESC + H
Q, T0, T1 = 60.0, 0.08, 0.25


def sigmoid(v):
    return 1.0 / (1.0 + np.exp(-v))


def draw_theta():
    sc = np.where(np.arange(K) == 0, T0, T1)[:, None, None]
    return bf((sc * np.random.standard_normal((K, P, H))).reshape(K * P, H))


def conv(xd, zd, theta, bias):
    cat = np.concatenate([np.concatenate([a.reshape(B, DESC, N), z.reshape(B, H, N)], axis=1) for a, z in zip(xd, zd)], axis=1)
    return (np.einsum("qh,bqn->bhn", f64(theta), cat) + f64(bias)[None]).reshape(B * H, N)


def setup_inputs():
    return {
        "x": bf(0.5 * np.random.standard_normal((B * DESC, N))),
        "state": f32(np.random.standard_normal((B * H, N))),
        "adj": f32(np.exp(-Q * np.random.random_sample((N, N)))),
        "theta_r": draw_theta(),
        "theta_u": draw_theta(),
        "theta_c": draw_theta(),
        "bias_r": f32(0.5 * np.random.standard_normal((H, 1))),
        "bias_u": f32(0.5 * np.random.standard_normal((H, 1))),
        "bias_c": f32(0.5 * np.random.standard_normal((H, 1))),
        "base": f32(np.random.standard_normal((B * H, S))),
        "offs": striped(np.random.permutation(S)[:N]),
    }


def reference(x, state, adj, theta_r, theta_u, theta_c, bias_r, bias_u, bias_c, base, offs):
    idx = offs[:16].T.reshape(-1)
    a = f64(adj)
    w1 = a / a.sum(axis=1, keepdims=True)
    w2 = a.T / a.sum(axis=0)[:, None]
    xv, hv = f64(x), f64(state)
    both = np.concatenate([xv, hv], axis=0)
    b1, b2 = both @ w1, both @ w2
    xd = [xv, b1[:B * DESC], b2[:B * DESC]]
    hd = [hv, b1[B * DESC:], b2[B * DESC:]]
    r = sigmoid(conv(xd, hd, theta_r, bias_r))
    u = sigmoid(conv(xd, hd, theta_u, bias_u))
    rh = r * hv
    cand = np.tanh(conv(xd, [rh, rh @ w1, rh @ w2], theta_c, bias_c))
    res = f64(base).copy()
    res[:, idx] = u * hv + (1.0 - u) * cand
    return res

@@ -1,0 +1,225 @@
+import concourse.mybir as mybir
+from concourse.masks import make_identity
+
+P = 128
+B = 3
+K = 3
+NODES = 1024
+STORE = 2048
+NB = NODES // P
+HALF = 512
+HALVES = NODES // HALF
+
+FLOPS = 2 * 3 * B * P * NODES * NODES * 2 + 2 * 3 * B * (2 * K * P) * P * NODES
+
+BF16, F32, U16 = mybir.dt.bfloat16, mybir.dt.float32, mybir.dt.uint16
+MULT, ADD = mybir.AluOpType.mult, mybir.AluOpType.add
+COPY = mybir.ActivationFunctionType.Copy
+SIGMOID = mybir.ActivationFunctionType.Sigmoid
+TANH = mybir.ActivationFunctionType.Tanh
+
+
+def tile_dcrnncell_b_kernel(
+    tc, x, state, adj, theta_r, theta_u, theta_c, bias_r, bias_u, bias_c, base, offs, out
+):
+    nc = tc.nc
+    with (
+        tc.tile_pool(name="held", bufs=1) as held,
+        tc.psum_pool(name="sums", bufs=6) as sums,
+        tc.psum_pool(name="turned", bufs=2) as turned,
+    ):
+        offsets = held.tile([P, NODES // 16], U16, name="offsets")
+        nc.sync.dma_start(offsets[:], offs)
+
+        def load_rows(pool, source, columns, dtype, name, block):
+            rows = pool.tile([P, columns], dtype, name=f"{name}{block}")
+            nc.sync.dma_start(rows[:], source[block * P : (block + 1) * P, :])
+            return rows
+
+        def load_theta(theta, bias, name):
+            weights = held.tile([P, 2 * K, P], BF16, name=f"theta_{name}")
+            nc.scalar.dma_start(weights[:], theta.rearrange("(q p) h -> p q h", p=P))
+            shift = held.tile([P, 1], F32, name=f"bias_{name}")
+            with nc.allow_non_contiguous_dma(reason="one float32 of the bias to each partition"):
+                nc.scalar.dma_start(shift[:], bias)
+            return weights, shift
+
+        def flip(rows, pool, name):
+            bank = turned.tile([P, NB, P], BF16, name="flip_bank", tag="turned")
+            for kb in range(NB):
+                nc.tensor.transpose(bank[:, kb, :], rows[:, kb * P : (kb + 1) * P], ident_bf[:])
+            flipped = pool.tile([P, NB, P], BF16, name=name)
+            nc.vector.tensor_copy(flipped[:], bank[:])
+            return flipped
+
+        def open_sums(row_blocks):
+            return [
+                [sums.tile([P, HALF], F32, name=f"sum{rb}{half}", tag="sum") for half in range(HALVES)]
+                for rb in range(row_blocks)
+            ]
+
+        def diffuse_step(banks, flipped, w_block, kb):
+            for rb in range(len(banks)):
+                for half in range(HALVES):
+                    nc.tensor.matmul(
+                        banks[rb][half][:],
+                        flipped[rb][:, kb, :],
+                        w_block[:, half * HALF : (half + 1) * HALF],
+                        start=kb == 0,
+                        stop=kb == NB - 1,
+                    )
+
+        def close_sums(banks, pool, name, share_with_vector):
+            rounded = []
+            for rb in range(len(banks)):
+                rows = pool.tile([P, NODES], BF16, name=f"{name}{rb}")
+                for half in range(HALVES):
+                    columns = rows[:, half * HALF : (half + 1) * HALF]
+                    if share_with_vector and half == 0:
+                        nc.vector.tensor_copy(columns, banks[rb][half][:])
+                    else:
+                        nc.scalar.copy(columns, banks[rb][half][:])
+                rounded.append(rows)
+            return rounded
+
+        def convolve(weights, inputs, hidden, half):
+            terms = [(2 * k, inputs[k]) for k in range(K)] + [(2 * k + 1, hidden[k]) for k in range(K)]
+            bank = sums.tile([P, HALF], F32, name="conv_bank", tag="sum")
+            for n, (q, rows) in enumerate(terms):
+                nc.tensor.matmul(
+                    bank[:],
+                    weights[:, q, :],
+                    rows[:, half * HALF : (half + 1) * HALF],
+                    start=n == 0,
+                    stop=n == len(terms) - 1,
+                )
+            return bank
+
+        x_rows = [load_rows(held, x, NODES, BF16, "x", b) for b in range(B)]
+        w_r, b_r = load_theta(theta_r, bias_r, "r")
+        w_u, b_u = load_theta(theta_u, bias_u, "u")
+        w_c, b_c = load_theta(theta_c, bias_c, "c")
+
+        ident_bf = held.tile([P, P], BF16, name="ident_bf")
+        make_identity(nc, ident_bf[:])
+        ident_f32 = held.tile([P, P], F32, name="ident_f32")
+        make_identity(nc, ident_f32[:])
+
+        w1 = [held.tile([P, NODES], BF16, name=f"w1_{kb}") for kb in range(NB)]
+        w2 = [held.tile([P, NODES], BF16, name=f"w2_{kb}") for kb in range(NB)]
+
+        with (
+            tc.tile_pool(name="graph", bufs=1) as graph,
+            tc.tile_pool(name="staging", bufs=2) as staging,
+            tc.tile_pool(name="stats", bufs=4) as stats,
+        ):
+            adj_rows = [load_rows(graph, adj, NODES, F32, "adj", kb) for kb in range(NB)]
+            state_rows = [load_rows(held, state, NODES, F32, "state", b) for b in range(B)]
+            window = [load_rows(held, base, STORE, F32, "window", b) for b in range(B)]
+
+            x_flipped = [flip(x_rows[b], held, f"x_flipped{b}") for b in range(B)]
+
+            for kb in range(NB):
+                total = stats.tile([P, 1], F32, name="row_total")
+                nc.vector.reduce_sum(total[:], adj_rows[kb][:], axis=mybir.AxisListType.X)
+                share = stats.tile([P, 1], F32, name="row_share")
+                nc.vector.reciprocal(share[:], total[:])
+                nc.scalar.activation(w1[kb][:], adj_rows[kb][:], COPY, scale=share[:, 0:1])
+
+            state_bf = []
+            for b in range(B):
+                rounded_state = held.tile([P, NODES], BF16, name=f"state_bf{b}")
+                nc.vector.tensor_copy(rounded_state[:], state_rows[b][:])
+                state_bf.append(rounded_state)
+
+            state_flipped = []
+            banks = open_sums(B)
+            for kb in range(NB):
+                if kb >= NB - B:
+                    b = kb - (NB - B)
+                    state_flipped.append(flip(state_bf[b], held, f"state_flipped{b}"))
+                diffuse_step(banks, x_flipped, w1[kb], kb)
+            d1_x = close_sums(banks, held, "d1_x", True)
+
+            banks = open_sums(B)
+            for kb in range(NB):
+                turned_rows = staging.tile([P, NODES], F32, name="turned_rows")
+                parts = stats.tile([P, HALVES], F32, name="column_parts")
+                for half in range(HALVES):
+                    bank = turned.tile([P, HALF], F32, name="adj_bank", tag="turned")
+                    for j in range(HALF // P):
+                        nc.tensor.transpose(
+                            bank[:, j * P : (j + 1) * P],
+                            adj_rows[half * (HALF // P) + j][:, kb * P : (kb + 1) * P],
+                            ident_f32[:],
+                        )
+                    nc.scalar.activation(
+                        turned_rows[:, half * HALF : (half + 1) * HALF],
+                        bank[:],
+                        COPY,
+                        accum_out=parts[:, half : half + 1],
+                    )
+                total = stats.tile([P, 1], F32, name="column_total")
+                nc.vector.reduce_sum(total[:], parts[:], axis=mybir.AxisListType.X)
+                share = stats.tile([P, 1], F32, name="column_share")
+                nc.vector.reciprocal(share[:], total[:])
+                nc.vector.tensor_scalar_mul(w2[kb][:], turned_rows[:], share[:, 0:1])
+
+                diffuse_step(banks, state_flipped, w1[kb], kb)
+            d1_state = close_sums(banks, held, "d1_state", True)
+
+        banks = open_sums(B)
+        for kb in range(NB):
+            diffuse_step(banks, x_flipped, w2[kb], kb)
+        d2_x = close_sums(banks, held, "d2_x", True)
+        banks = open_sums(B)
+        for kb in range(NB):
+            diffuse_step(banks, state_flipped, w2[kb], kb)
+        d2_state = close_sums(banks, held, "d2_state", True)
+
+        with (
+            tc.tile_pool(name="gates", bufs=1) as gates,
+            tc.tile_pool(name="work", bufs=3) as work,
+        ):
+            reset_rows = []
+            for b in range(B):
+                rows = gates.tile([P, NODES], BF16, name=f"reset_rows{b}")
+                for half in range(HALVES):
+                    columns = slice(half * HALF, (half + 1) * HALF)
+                    bank = convolve(w_r, [x_rows[b], d1_x[b], d2_x[b]], [state_bf[b], d1_state[b], d2_state[b]], half)
+                    r = work.tile([P, HALF], F32, name="r")
+                    nc.scalar.activation(r[:], bank[:], SIGMOID, bias=b_r[:, 0:1])
+                    nc.vector.tensor_tensor(rows[:, columns], r[:], state_rows[b][:, columns], MULT)
+                reset_rows.append(rows)
+
+            reset_flipped, keep, rest = [], [], []
+            for b in range(B):
+                reset_flipped.append(flip(reset_rows[b], gates, f"reset_flipped{b}"))
+                kept = gates.tile([P, NODES], F32, name=f"keep{b}")
+                left = gates.tile([P, NODES], F32, name=f"rest{b}")
+                for half in range(HALVES):
+                    columns = slice(half * HALF, (half + 1) * HALF)
+                    bank = convolve(w_u, [x_rows[b], d1_x[b], d2_x[b]], [state_bf[b], d1_state[b], d2_state[b]], half)
+                    u = work.tile([P, HALF], F32, name="u")
+                    nc.scalar.activation(u[:], bank[:], SIGMOID, bias=b_u[:, 0:1])
+                    nc.vector.tensor_tensor(kept[:, columns], u[:], state_rows[b][:, columns], MULT)
+                    nc.vector.tensor_scalar(left[:, columns], u[:], -1.0, 1.0, MULT, ADD)
+                keep.append(kept)
+                rest.append(left)
+
+            for b in range(B):
+                spread = []
+                for w, name in ((w1, "d1_reset"), (w2, "d2_reset")):
+                    banks = open_sums(1)
+                    for kb in range(NB):
+                        diffuse_step(banks, [reset_flipped[b]], w[kb], kb)
+                    spread.append(close_sums(banks, gates, f"{name}{b}_", False)[0])
+                fresh = gates.tile([P, NODES], F32, name=f"fresh{b}")
+                for half in range(HALVES):
+                    columns = slice(half * HALF, (half + 1) * HALF)
+                    bank = convolve(w_c, [x_rows[b], d1_x[b], d2_x[b]], [reset_rows[b], spread[0], spread[1]], half)
+                    cand = work.tile([P, HALF], F32, name="cand")
+                    nc.scalar.activation(cand[:], bank[:], TANH, bias=b_c[:, 0:1])
+                    nc.vector.tensor_tensor(fresh[:, columns], rest[b][:, columns], cand[:], MULT)
+                nc.vector.tensor_tensor(window[b][:].indirect(offsets[:]), keep[b][:], fresh[:], ADD)
+                nc.sync.dma_start(out[b * P : (b + 1) * P, :], window[b][:])

@@ -52,18 +52,32 @@ def tile_dcrnncell_b_kernel(
             nc.vector.tensor_copy(flipped[:], bank[:])
             return flipped
 
+        def flip_block(samples, kb, name):
+            bank = turned.tile([P, B * P], BF16, name="block_bank", tag="turned")
+            for b in range(B):
+                nc.tensor.transpose(bank[:, b * P : (b + 1) * P], samples[b][:, kb * P : (kb + 1) * P], ident_bf[:])
+            flipped = held.tile([P, B * P], BF16, name=f"{name}{kb}")
+            nc.scalar.copy(flipped[:], bank[:])
+            return flipped
+
+        def samples_of(flipped_block):
+            return [flipped_block[:, b * P : (b + 1) * P] for b in range(B)]
+
+        def blocks_of(flipped_samples, kb):
+            return [flipped[:, kb, :] for flipped in flipped_samples]
+
         def open_sums(row_blocks):
             return [
                 [sums.tile([P, HALF], F32, name=f"sum{rb}{half}", tag="sum") for half in range(HALVES)]
                 for rb in range(row_blocks)
             ]
 
-        def diffuse_step(banks, flipped, w_block, kb):
+        def diffuse_step(banks, stationary, w_block, kb):
             for rb in range(len(banks)):
                 for half in range(HALVES):
                     nc.tensor.matmul(
                         banks[rb][half][:],
-                        flipped[rb][:, kb, :],
+                        stationary[rb],
                         w_block[:, half * HALF : (half + 1) * HALF],
                         start=kb == 0,
                         stop=kb == NB - 1,
@@ -95,7 +109,6 @@ def tile_dcrnncell_b_kernel(
                 )
             return bank
 
-        x_rows = [load_rows(held, x, NODES, BF16, "x", b) for b in range(B)]
         w_r, b_r = load_theta(theta_r, bias_r, "r")
         w_u, b_u = load_theta(theta_u, bias_u, "u")
         w_c, b_c = load_theta(theta_c, bias_c, "c")
@@ -113,13 +126,13 @@ def tile_dcrnncell_b_kernel(
             tc.tile_pool(name="staging", bufs=2) as staging,
             tc.tile_pool(name="stats", bufs=4) as stats,
         ):
-            adj_rows = [load_rows(graph, adj, NODES, F32, "adj", kb) for kb in range(NB)]
+            adj_rows = [load_rows(graph, adj, NODES, F32, "adj", 0)]
+            x_rows = [load_rows(held, x, NODES, BF16, "x", b) for b in range(B)]
+            adj_rows += [load_rows(graph, adj, NODES, F32, "adj", kb) for kb in range(1, NB)]
             state_rows = [load_rows(held, state, NODES, F32, "state", b) for b in range(B)]
             window = [load_rows(held, base, STORE, F32, "window", b) for b in range(B)]
 
-            x_flipped = [flip(x_rows[b], held, f"x_flipped{b}") for b in range(B)]
-
-            for kb in range(NB):
+            def normalise_rows(kb):
                 total = stats.tile([P, 1], F32, name="row_total")
                 nc.vector.reduce_sum(total[:], adj_rows[kb][:], axis=mybir.AxisListType.X)
                 share = stats.tile([P, 1], F32, name="row_share")
@@ -129,16 +142,21 @@ def tile_dcrnncell_b_kernel(
             state_bf = []
             for b in range(B):
                 rounded_state = held.tile([P, NODES], BF16, name=f"state_bf{b}")
-                nc.vector.tensor_copy(rounded_state[:], state_rows[b][:])
+                nc.gpsimd.tensor_copy(rounded_state[:], state_rows[b][:])
                 state_bf.append(rounded_state)
 
+            normalise_rows(0)
+            x_flipped = [flip_block(x_rows, 0, "x_flipped")]
             state_flipped = []
             banks = open_sums(B)
             for kb in range(NB):
+                if kb + 1 < NB:
+                    normalise_rows(kb + 1)
+                    x_flipped.append(flip_block(x_rows, kb + 1, "x_flipped"))
                 if kb >= NB - B:
                     b = kb - (NB - B)
                     state_flipped.append(flip(state_bf[b], held, f"state_flipped{b}"))
-                diffuse_step(banks, x_flipped, w1[kb], kb)
+                diffuse_step(banks, samples_of(x_flipped[kb]), w1[kb], kb)
             d1_x = close_sums(banks, held, "d1_x", True)
 
             banks = open_sums(B)
@@ -165,16 +183,16 @@ def tile_dcrnncell_b_kernel(
                 nc.vector.reciprocal(share[:], total[:])
                 nc.vector.tensor_scalar_mul(w2[kb][:], turned_rows[:], share[:, 0:1])
 
-                diffuse_step(banks, state_flipped, w1[kb], kb)
+                diffuse_step(banks, blocks_of(state_flipped, kb), w1[kb], kb)
             d1_state = close_sums(banks, held, "d1_state", True)
 
         banks = open_sums(B)
         for kb in range(NB):
-            diffuse_step(banks, x_flipped, w2[kb], kb)
+            diffuse_step(banks, samples_of(x_flipped[kb]), w2[kb], kb)
         d2_x = close_sums(banks, held, "d2_x", True)
         banks = open_sums(B)
         for kb in range(NB):
-            diffuse_step(banks, state_flipped, w2[kb], kb)
+            diffuse_step(banks, blocks_of(state_flipped, kb), w2[kb], kb)
         d2_state = close_sums(banks, held, "d2_state", True)
 
         with (
@@ -212,7 +230,7 @@ def tile_dcrnncell_b_kernel(
                 for w, name in ((w1, "d1_reset"), (w2, "d2_reset")):
                     banks = open_sums(1)
                     for kb in range(NB):
-                        diffuse_step(banks, [reset_flipped[b]], w[kb], kb)
+                        diffuse_step(banks, blocks_of([reset_flipped[b]], kb), w[kb], kb)
                     spread.append(close_sums(banks, gates, f"{name}{b}_", False)[0])
                 fresh = gates.tile([P, NODES], F32, name=f"fresh{b}")
                 for half in range(HALVES):

@@ -96,6 +96,12 @@ def tile_dcrnncell_b_kernel(
                 rounded.append(rows)
             return rounded
 
+        def diffuse_sample(stationary_blocks, w, pool, name, share_with_vector):
+            banks = open_sums(1)
+            for kb in range(NB):
+                diffuse_step(banks, [stationary_blocks[kb]], w[kb], kb)
+            return close_sums(banks, pool, name, share_with_vector)[0]
+
         def convolve(weights, inputs, hidden, half):
             terms = [(2 * k, inputs[k]) for k in range(K)] + [(2 * k + 1, hidden[k]) for k in range(K)]
             bank = sums.tile([P, HALF], F32, name="conv_bank", tag="sum")
@@ -186,14 +192,14 @@ def tile_dcrnncell_b_kernel(
                 diffuse_step(banks, blocks_of(state_flipped, kb), w1[kb], kb)
             d1_state = close_sums(banks, held, "d1_state", True)
 
-        banks = open_sums(B)
-        for kb in range(NB):
-            diffuse_step(banks, samples_of(x_flipped[kb]), w2[kb], kb)
-        d2_x = close_sums(banks, held, "d2_x", True)
-        banks = open_sums(B)
-        for kb in range(NB):
-            diffuse_step(banks, blocks_of(state_flipped, kb), w2[kb], kb)
-        d2_state = close_sums(banks, held, "d2_state", True)
+        d2_x = [
+            diffuse_sample([samples_of(x_flipped[kb])[b] for kb in range(NB)], w2, held, f"d2_x{b}_", True)
+            for b in range(B)
+        ]
+        d2_state = [
+            diffuse_sample([state_flipped[b][:, kb, :] for kb in range(NB)], w2, held, f"d2_state{b}_", True)
+            for b in range(B)
+        ]
 
         with (
             tc.tile_pool(name="gates", bufs=1) as gates,
@@ -226,12 +232,11 @@ def tile_dcrnncell_b_kernel(
                 rest.append(left)
 
             for b in range(B):
-                spread = []
-                for w, name in ((w1, "d1_reset"), (w2, "d2_reset")):
-                    banks = open_sums(1)
-                    for kb in range(NB):
-                        diffuse_step(banks, blocks_of([reset_flipped[b]], kb), w[kb], kb)
-                    spread.append(close_sums(banks, gates, f"{name}{b}_", False)[0])
+                reset_blocks = [reset_flipped[b][:, kb, :] for kb in range(NB)]
+                spread = [
+                    diffuse_sample(reset_blocks, w1, gates, f"d1_reset{b}_", False),
+                    diffuse_sample(reset_blocks, w2, gates, f"d2_reset{b}_", False),
+                ]
                 fresh = gates.tile([P, NODES], F32, name=f"fresh{b}")
                 for half in range(HALVES):
                     columns = slice(half * HALF, (half + 1) * HALF)

@@ -9,6 +9,8 @@ STORE = 2048
 NB = NODES // P
 HALF = 512
 HALVES = NODES // HALF
+R, U, C = 0, 1, 2
+GATES = 3
 
 FLOPS = 2 * 3 * B * P * NODES * NODES * 2 + 2 * 3 * B * (2 * K * P) * P * NODES
 
@@ -25,224 +27,182 @@ def tile_dcrnncell_b_kernel(
     nc = tc.nc
     with (
         tc.tile_pool(name="held", bufs=1) as held,
-        tc.psum_pool(name="sums", bufs=6) as sums,
-        tc.psum_pool(name="turned", bufs=2) as turned,
+        tc.tile_pool(name="staging", bufs=2) as staging,
+        tc.tile_pool(name="stats", bufs=4) as stats,
+        tc.tile_pool(name="work", bufs=3) as work,
+        tc.psum_pool(name="banks", bufs=8) as banks,
     ):
-        offsets = held.tile([P, NODES // 16], U16, name="offsets")
-        nc.sync.dma_start(offsets[:], offs)
+        theta_in = held.tile([P, K, GATES * P], BF16, name="theta_in")
+        theta_hid = held.tile([P, K, GATES * P], BF16, name="theta_hid")
 
-        def load_rows(pool, source, columns, dtype, name, block):
-            rows = pool.tile([P, columns], dtype, name=f"{name}{block}")
-            nc.sync.dma_start(rows[:], source[block * P : (block + 1) * P, :])
-            return rows
+        def load_theta(theta, g):
+            blocks = theta.rearrange("(k z p) h -> z p k h", z=2, p=P)
+            nc.sync.dma_start(theta_in[:, :, g * P : (g + 1) * P], blocks[0, :, :, :])
+            nc.sync.dma_start(theta_hid[:, :, g * P : (g + 1) * P], blocks[1, :, :, :])
 
-        def load_theta(theta, bias, name):
-            weights = held.tile([P, 2 * K, P], BF16, name=f"theta_{name}")
-            nc.scalar.dma_start(weights[:], theta.rearrange("(q p) h -> p q h", p=P))
+        def load_bias(bias, name):
             shift = held.tile([P, 1], F32, name=f"bias_{name}")
             with nc.allow_non_contiguous_dma(reason="one float32 of the bias to each partition"):
                 nc.scalar.dma_start(shift[:], bias)
-            return weights, shift
+            return shift
 
-        def flip(rows, pool, name):
-            bank = turned.tile([P, NB, P], BF16, name="flip_bank", tag="turned")
-            for kb in range(NB):
-                nc.tensor.transpose(bank[:, kb, :], rows[:, kb * P : (kb + 1) * P], ident_bf[:])
-            flipped = pool.tile([P, NB, P], BF16, name=name)
-            nc.vector.tensor_copy(flipped[:], bank[:])
-            return flipped
+        def load_rows(source, columns, dtype, name, block):
+            rows = held.tile([P, columns], dtype, name=f"{name}{block}")
+            nc.sync.dma_start(rows[:], source[block * P : (block + 1) * P, :])
+            return rows
 
-        def flip_block(samples, kb, name):
-            bank = turned.tile([P, B * P], BF16, name="block_bank", tag="turned")
-            for b in range(B):
-                nc.tensor.transpose(bank[:, b * P : (b + 1) * P], samples[b][:, kb * P : (kb + 1) * P], ident_bf[:])
-            flipped = held.tile([P, B * P], BF16, name=f"{name}{kb}")
-            nc.scalar.copy(flipped[:], bank[:])
-            return flipped
+        load_theta(theta_r, R)
+        load_theta(theta_u, U)
+        x_rows, state_rows = [], []
+        for b in range(B):
+            x_rows.append(load_rows(x, NODES, BF16, "x", b))
+            state_rows.append(load_rows(state, NODES, F32, "state", b))
+        load_theta(theta_c, C)
+        adj_rows = [load_rows(adj, NODES, F32, "adj", kb) for kb in range(NB)]
+        offsets = held.tile([P, NODES // 16], U16, name="offsets")
+        nc.sync.dma_start(offsets[:], offs)
+        window = [load_rows(base, STORE, F32, "window", b) for b in range(B)]
+        b_r, b_u, b_c = load_bias(bias_r, "r"), load_bias(bias_u, "u"), load_bias(bias_c, "c")
 
-        def samples_of(flipped_block):
-            return [flipped_block[:, b * P : (b + 1) * P] for b in range(B)]
-
-        def blocks_of(flipped_samples, kb):
-            return [flipped[:, kb, :] for flipped in flipped_samples]
-
-        def open_sums(row_blocks):
-            return [
-                [sums.tile([P, HALF], F32, name=f"sum{rb}{half}", tag="sum") for half in range(HALVES)]
-                for rb in range(row_blocks)
-            ]
-
-        def diffuse_step(banks, stationary, w_block, kb):
-            for rb in range(len(banks)):
-                for half in range(HALVES):
-                    nc.tensor.matmul(
-                        banks[rb][half][:],
-                        stationary[rb],
-                        w_block[:, half * HALF : (half + 1) * HALF],
-                        start=kb == 0,
-                        stop=kb == NB - 1,
-                    )
-
-        def close_sums(banks, pool, name, share_with_vector):
-            rounded = []
-            for rb in range(len(banks)):
-                rows = pool.tile([P, NODES], BF16, name=f"{name}{rb}")
-                for half in range(HALVES):
-                    columns = rows[:, half * HALF : (half + 1) * HALF]
-                    if share_with_vector and half == 0:
-                        nc.vector.tensor_copy(columns, banks[rb][half][:])
-                    else:
-                        nc.scalar.copy(columns, banks[rb][half][:])
-                rounded.append(rows)
-            return rounded
-
-        def diffuse_sample(stationary_blocks, w, pool, name, share_with_vector):
-            banks = open_sums(1)
-            for kb in range(NB):
-                diffuse_step(banks, [stationary_blocks[kb]], w[kb], kb)
-            return close_sums(banks, pool, name, share_with_vector)[0]
-
-        def convolve(weights, inputs, hidden, half):
-            terms = [(2 * k, inputs[k]) for k in range(K)] + [(2 * k + 1, hidden[k]) for k in range(K)]
-            bank = sums.tile([P, HALF], F32, name="conv_bank", tag="sum")
-            for n, (q, rows) in enumerate(terms):
-                nc.tensor.matmul(
-                    bank[:],
-                    weights[:, q, :],
-                    rows[:, half * HALF : (half + 1) * HALF],
-                    start=n == 0,
-                    stop=n == len(terms) - 1,
-                )
-            return bank
-
-        w_r, b_r = load_theta(theta_r, bias_r, "r")
-        w_u, b_u = load_theta(theta_u, bias_u, "u")
-        w_c, b_c = load_theta(theta_c, bias_c, "c")
-
-        ident_bf = held.tile([P, P], BF16, name="ident_bf")
-        make_identity(nc, ident_bf[:])
         ident_f32 = held.tile([P, P], F32, name="ident_f32")
         make_identity(nc, ident_f32[:])
 
+        def empty(rounded, bank, turn):
+            if turn % 2 == 0:
+                nc.scalar.copy(rounded[:], bank[:])
+            else:
+                nc.vector.tensor_copy(rounded[:], bank[:])
+
+        def columns_of(half):
+            return slice(half * HALF, (half + 1) * HALF)
+
+        def nodes_of(kb):
+            return slice(kb * P, (kb + 1) * P)
+
+        state_bf = []
+        for b in range(B):
+            rounded_state = held.tile([P, NODES], BF16, name=f"state_bf{b}")
+            nc.vector.tensor_copy(rounded_state[:], state_rows[b][:])
+            state_bf.append(rounded_state)
+
+        mixed = []
+        for b in range(B):
+            blocks = []
+            for kb in range(NB):
+                bank = banks.tile([P, 2, 2 * P], F32, name="mix_bank", tag="bank")
+                nc.tensor.matmul(
+                    bank[:], x_rows[b][:, nodes_of(kb)], theta_in[:, 1:K, 0 : 2 * P], start=True, stop=False
+                )
+                nc.tensor.matmul(
+                    bank[:], state_bf[b][:, nodes_of(kb)], theta_hid[:, 1:K, 0 : 2 * P], start=False, stop=True
+                )
+                rounded = held.tile([P, 2, 2 * P], BF16, name=f"mixed{b}_{kb}")
+                empty(rounded, bank, kb)
+                blocks.append(rounded)
+            mixed.append(blocks)
+
         w1 = [held.tile([P, NODES], BF16, name=f"w1_{kb}") for kb in range(NB)]
         w2 = [held.tile([P, NODES], BF16, name=f"w2_{kb}") for kb in range(NB)]
+        w = [None, w1, w2]
+        for kb in range(NB):
+            total = stats.tile([P, 1], F32, name="row_total")
+            nc.vector.reduce_sum(total[:], adj_rows[kb][:], axis=mybir.AxisListType.X)
+            share = stats.tile([P, 1], F32, name="row_share")
+            nc.vector.reciprocal(share[:], total[:])
+            nc.scalar.activation(w1[kb][:], adj_rows[kb][:], COPY, scale=share[:, 0:1])
 
-        with (
-            tc.tile_pool(name="graph", bufs=1) as graph,
-            tc.tile_pool(name="staging", bufs=2) as staging,
-            tc.tile_pool(name="stats", bufs=4) as stats,
-        ):
-            adj_rows = [load_rows(graph, adj, NODES, F32, "adj", 0)]
-            x_rows = [load_rows(held, x, NODES, BF16, "x", b) for b in range(B)]
-            adj_rows += [load_rows(graph, adj, NODES, F32, "adj", kb) for kb in range(1, NB)]
-            state_rows = [load_rows(held, state, NODES, F32, "state", b) for b in range(B)]
-            window = [load_rows(held, base, STORE, F32, "window", b) for b in range(B)]
-
-            def normalise_rows(kb):
-                total = stats.tile([P, 1], F32, name="row_total")
-                nc.vector.reduce_sum(total[:], adj_rows[kb][:], axis=mybir.AxisListType.X)
-                share = stats.tile([P, 1], F32, name="row_share")
-                nc.vector.reciprocal(share[:], total[:])
-                nc.scalar.activation(w1[kb][:], adj_rows[kb][:], COPY, scale=share[:, 0:1])
-
-            state_bf = []
-            for b in range(B):
-                rounded_state = held.tile([P, NODES], BF16, name=f"state_bf{b}")
-                nc.gpsimd.tensor_copy(rounded_state[:], state_rows[b][:])
-                state_bf.append(rounded_state)
-
-            normalise_rows(0)
-            x_flipped = [flip_block(x_rows, 0, "x_flipped")]
-            state_flipped = []
-            banks = open_sums(B)
-            for kb in range(NB):
-                if kb + 1 < NB:
-                    normalise_rows(kb + 1)
-                    x_flipped.append(flip_block(x_rows, kb + 1, "x_flipped"))
-                if kb >= NB - B:
-                    b = kb - (NB - B)
-                    state_flipped.append(flip(state_bf[b], held, f"state_flipped{b}"))
-                diffuse_step(banks, samples_of(x_flipped[kb]), w1[kb], kb)
-            d1_x = close_sums(banks, held, "d1_x", True)
-
-            banks = open_sums(B)
-            for kb in range(NB):
-                turned_rows = staging.tile([P, NODES], F32, name="turned_rows")
-                parts = stats.tile([P, HALVES], F32, name="column_parts")
-                for half in range(HALVES):
-                    bank = turned.tile([P, HALF], F32, name="adj_bank", tag="turned")
-                    for j in range(HALF // P):
-                        nc.tensor.transpose(
-                            bank[:, j * P : (j + 1) * P],
-                            adj_rows[half * (HALF // P) + j][:, kb * P : (kb + 1) * P],
-                            ident_f32[:],
-                        )
-                    nc.scalar.activation(
-                        turned_rows[:, half * HALF : (half + 1) * HALF],
-                        bank[:],
-                        COPY,
-                        accum_out=parts[:, half : half + 1],
+        def turn_columns(kb):
+            turned_rows = staging.tile([P, NODES], F32, name="turned_rows")
+            parts = stats.tile([P, HALVES], F32, name="column_parts")
+            for half in range(HALVES):
+                bank = banks.tile([P, HALF], F32, name="adj_bank", tag="bank")
+                for j in range(HALF // P):
+                    nc.tensor.transpose(
+                        bank[:, nodes_of(j)], adj_rows[half * (HALF // P) + j][:, nodes_of(kb)], ident_f32[:]
                     )
-                total = stats.tile([P, 1], F32, name="column_total")
-                nc.vector.reduce_sum(total[:], parts[:], axis=mybir.AxisListType.X)
-                share = stats.tile([P, 1], F32, name="column_share")
-                nc.vector.reciprocal(share[:], total[:])
-                nc.vector.tensor_scalar_mul(w2[kb][:], turned_rows[:], share[:, 0:1])
+                nc.scalar.activation(
+                    turned_rows[:, columns_of(half)], bank[:], COPY, accum_out=parts[:, half : half + 1]
+                )
+            total = stats.tile([P, 1], F32, name="column_total")
+            nc.vector.reduce_sum(total[:], parts[:], axis=mybir.AxisListType.X)
+            share = stats.tile([P, 1], F32, name="column_share")
+            nc.vector.reciprocal(share[:], total[:])
+            nc.vector.tensor_scalar_mul(w2[kb][:], turned_rows[:], share[:, 0:1])
 
-                diffuse_step(banks, blocks_of(state_flipped, kb), w1[kb], kb)
-            d1_state = close_sums(banks, held, "d1_state", True)
+        def open_gate(g, b, half, hidden):
+            bank = banks.tile([P, HALF], F32, name="gate_bank", tag="bank")
+            weights = slice(g * P, (g + 1) * P)
+            nc.tensor.matmul(bank[:], theta_in[:, 0, weights], x_rows[b][:, columns_of(half)], start=True, stop=False)
+            nc.tensor.matmul(bank[:], theta_hid[:, 0, weights], hidden[b][:, columns_of(half)], start=False, stop=False)
+            return bank
 
-        d2_x = [
-            diffuse_sample([samples_of(x_flipped[kb])[b] for kb in range(NB)], w2, held, f"d2_x{b}_", True)
-            for b in range(B)
-        ]
-        d2_state = [
-            diffuse_sample([state_flipped[b][:, kb, :] for kb in range(NB)], w2, held, f"d2_state{b}_", True)
-            for b in range(B)
-        ]
+        def diffuse(bank, mixed_block, k, kb, half):
+            nc.tensor.matmul(
+                bank[:], mixed_block, w[k][kb][:, columns_of(half)], start=False, stop=k == K - 1 and kb == NB - 1
+            )
 
-        with (
-            tc.tile_pool(name="gates", bufs=1) as gates,
-            tc.tile_pool(name="work", bufs=3) as work,
-        ):
-            reset_rows = []
+        turn_columns(0)
+        r_banks = [[open_gate(R, b, half, state_bf) for half in range(HALVES)] for b in range(B)]
+        for kb in range(NB):
+            if kb + 1 < NB:
+                turn_columns(kb + 1)
             for b in range(B):
-                rows = gates.tile([P, NODES], BF16, name=f"reset_rows{b}")
                 for half in range(HALVES):
-                    columns = slice(half * HALF, (half + 1) * HALF)
-                    bank = convolve(w_r, [x_rows[b], d1_x[b], d2_x[b]], [state_bf[b], d1_state[b], d2_state[b]], half)
-                    r = work.tile([P, HALF], F32, name="r")
-                    nc.scalar.activation(r[:], bank[:], SIGMOID, bias=b_r[:, 0:1])
-                    nc.vector.tensor_tensor(rows[:, columns], r[:], state_rows[b][:, columns], MULT)
-                reset_rows.append(rows)
+                    diffuse(r_banks[b][half], mixed[b][kb][:, 0, R * P : (R + 1) * P], 1, kb, half)
+        reset_rows = [held.tile([P, NODES], BF16, name=f"reset_rows{b}") for b in range(B)]
+        for b in range(B):
+            for half in range(HALVES):
+                for kb in range(NB):
+                    diffuse(r_banks[b][half], mixed[b][kb][:, 1, R * P : (R + 1) * P], 2, kb, half)
+                r = work.tile([P, HALF], F32, name="r")
+                nc.scalar.activation(r[:], r_banks[b][half][:], SIGMOID, bias=b_r[:, 0:1])
+                nc.vector.tensor_tensor(
+                    reset_rows[b][:, columns_of(half)], r[:], state_rows[b][:, columns_of(half)], MULT
+                )
 
-            reset_flipped, keep, rest = [], [], []
-            for b in range(B):
-                reset_flipped.append(flip(reset_rows[b], gates, f"reset_flipped{b}"))
-                kept = gates.tile([P, NODES], F32, name=f"keep{b}")
-                left = gates.tile([P, NODES], F32, name=f"rest{b}")
-                for half in range(HALVES):
-                    columns = slice(half * HALF, (half + 1) * HALF)
-                    bank = convolve(w_u, [x_rows[b], d1_x[b], d2_x[b]], [state_bf[b], d1_state[b], d2_state[b]], half)
-                    u = work.tile([P, HALF], F32, name="u")
-                    nc.scalar.activation(u[:], bank[:], SIGMOID, bias=b_u[:, 0:1])
-                    nc.vector.tensor_tensor(kept[:, columns], u[:], state_rows[b][:, columns], MULT)
-                    nc.vector.tensor_scalar(left[:, columns], u[:], -1.0, 1.0, MULT, ADD)
-                keep.append(kept)
-                rest.append(left)
+        mixed_c, keep, rest = [], [], []
+        for b in range(B):
+            pairs = []
+            for pair in range(NB // 2):
+                bank = banks.tile([P, 2, 2, P], F32, name="mix_c_bank", tag="bank")
+                for j in range(2):
+                    nodes = nodes_of(2 * pair + j)
+                    nc.tensor.matmul(
+                        bank[:, j, :, :], x_rows[b][:, nodes], theta_in[:, 1:K, C * P : (C + 1) * P],
+                        start=True, stop=False,
+                    )
+                    nc.tensor.matmul(
+                        bank[:, j, :, :], reset_rows[b][:, nodes], theta_hid[:, 1:K, C * P : (C + 1) * P],
+                        start=False, stop=True,
+                    )
+                rounded = held.tile([P, 2, 2, P], BF16, name=f"mixed_c{b}_{pair}")
+                empty(rounded, bank, pair)
+                pairs.append(rounded)
+            mixed_c.append(pairs)
 
-            for b in range(B):
-                reset_blocks = [reset_flipped[b][:, kb, :] for kb in range(NB)]
-                spread = [
-                    diffuse_sample(reset_blocks, w1, gates, f"d1_reset{b}_", False),
-                    diffuse_sample(reset_blocks, w2, gates, f"d2_reset{b}_", False),
-                ]
-                fresh = gates.tile([P, NODES], F32, name=f"fresh{b}")
-                for half in range(HALVES):
-                    columns = slice(half * HALF, (half + 1) * HALF)
-                    bank = convolve(w_c, [x_rows[b], d1_x[b], d2_x[b]], [reset_rows[b], spread[0], spread[1]], half)
-                    cand = work.tile([P, HALF], F32, name="cand")
-                    nc.scalar.activation(cand[:], bank[:], TANH, bias=b_c[:, 0:1])
-                    nc.vector.tensor_tensor(fresh[:, columns], rest[b][:, columns], cand[:], MULT)
-                nc.vector.tensor_tensor(window[b][:].indirect(offsets[:]), keep[b][:], fresh[:], ADD)
-                nc.sync.dma_start(out[b * P : (b + 1) * P, :], window[b][:])
+            kept = held.tile([P, NODES], F32, name=f"keep{b}")
+            left = held.tile([P, NODES], F32, name=f"rest{b}")
+            for half in range(HALVES):
+                bank = open_gate(U, b, half, state_bf)
+                for k in range(1, K):
+                    for kb in range(NB):
+                        diffuse(bank, mixed[b][kb][:, k - 1, U * P : (U + 1) * P], k, kb, half)
+                u = work.tile([P, HALF], F32, name="u")
+                nc.scalar.activation(u[:], bank[:], SIGMOID, bias=b_u[:, 0:1])
+                nc.vector.tensor_tensor(kept[:, columns_of(half)], u[:], state_rows[b][:, columns_of(half)], MULT)
+                nc.vector.tensor_scalar(left[:, columns_of(half)], u[:], -1.0, 1.0, MULT, ADD)
+            keep.append(kept)
+            rest.append(left)
+
+        for b in range(B):
+            fresh = held.tile([P, NODES], F32, name=f"fresh{b}")
+            for half in range(HALVES):
+                bank = open_gate(C, b, half, reset_rows)
+                for k in range(1, K):
+                    for kb in range(NB):
+                        diffuse(bank, mixed_c[b][kb // 2][:, kb % 2, k - 1, :], k, kb, half)
+                cand = work.tile([P, HALF], F32, name="cand")
+                nc.scalar.activation(cand[:], bank[:], TANH, bias=b_c[:, 0:1])
+                nc.vector.tensor_tensor(fresh[:, columns_of(half)], rest[b][:, columns_of(half)], cand[:], MULT)
+            nc.vector.tensor_tensor(window[b][:].indirect(offsets[:]), keep[b][:], fresh[:], ADD)
+            nc.sync.dma_start(out[b * P : (b + 1) * P, :], window[b][:])

@@ -11,6 +11,7 @@ HALF = 512
 HALVES = NODES // HALF
 R, U, C = 0, 1, 2
 GATES = 3
+TURNS = NB * NB
 
 FLOPS = 2 * 3 * B * P * NODES * NODES * 2 + 2 * 3 * B * (2 * K * P) * P * NODES
 
@@ -111,29 +112,41 @@ def tile_dcrnncell_b_kernel(
             nc.vector.reciprocal(share[:], total[:])
             nc.scalar.activation(w1[kb][:], adj_rows[kb][:], COPY, scale=share[:, 0:1])
 
-        def turn_columns(kb):
-            turned_rows = staging.tile([P, NODES], F32, name="turned_rows")
-            parts = stats.tile([P, HALVES], F32, name="column_parts")
-            for half in range(HALVES):
-                bank = banks.tile([P, HALF], F32, name="adj_bank", tag="bank")
-                for j in range(HALF // P):
-                    nc.tensor.transpose(
-                        bank[:, nodes_of(j)], adj_rows[half * (HALF // P) + j][:, nodes_of(kb)], ident_f32[:]
-                    )
+        making = {}
+
+        def turn(n):
+            kb, piece = divmod(n, NB)
+            half, j = divmod(piece, HALF // P)
+            if piece == 0:
+                making["rows"] = staging.tile([P, NODES], F32, name="turned_rows")
+                making["parts"] = stats.tile([P, HALVES], F32, name="column_parts")
+            if j == 0:
+                making["bank"] = banks.tile([P, HALF], F32, name="adj_bank", tag="bank")
+            nc.tensor.transpose(making["bank"][:, nodes_of(j)], adj_rows[piece][:, nodes_of(kb)], ident_f32[:])
+            if j == HALF // P - 1:
                 nc.scalar.activation(
-                    turned_rows[:, columns_of(half)], bank[:], COPY, accum_out=parts[:, half : half + 1]
+                    making["rows"][:, columns_of(half)],
+                    making["bank"][:],
+                    COPY,
+                    accum_out=making["parts"][:, half : half + 1],
                 )
-            total = stats.tile([P, 1], F32, name="column_total")
-            nc.vector.reduce_sum(total[:], parts[:], axis=mybir.AxisListType.X)
-            share = stats.tile([P, 1], F32, name="column_share")
-            nc.vector.reciprocal(share[:], total[:])
-            nc.vector.tensor_scalar_mul(w2[kb][:], turned_rows[:], share[:, 0:1])
+            if piece == NB - 1:
+                total = stats.tile([P, 1], F32, name="column_total")
+                nc.vector.reduce_sum(total[:], making["parts"][:], axis=mybir.AxisListType.X)
+                share = stats.tile([P, 1], F32, name="column_share")
+                nc.vector.reciprocal(share[:], total[:])
+                nc.vector.tensor_scalar_mul(w2[kb][:], making["rows"][:], share[:, 0:1])
+
+        def direct(bank, g, b, half, z, hidden):
+            weights, rows = ((theta_in, x_rows), (theta_hid, hidden))[z]
+            nc.tensor.matmul(
+                bank[:], weights[:, 0, g * P : (g + 1) * P], rows[b][:, columns_of(half)], start=z == 0, stop=False
+            )
 
         def open_gate(g, b, half, hidden):
             bank = banks.tile([P, HALF], F32, name="gate_bank", tag="bank")
-            weights = slice(g * P, (g + 1) * P)
-            nc.tensor.matmul(bank[:], theta_in[:, 0, weights], x_rows[b][:, columns_of(half)], start=True, stop=False)
-            nc.tensor.matmul(bank[:], theta_hid[:, 0, weights], hidden[b][:, columns_of(half)], start=False, stop=False)
+            for z in range(2):
+                direct(bank, g, b, half, z, hidden)
             return bank
 
         def diffuse(bank, mixed_block, k, kb, half):
@@ -141,27 +154,43 @@ def tile_dcrnncell_b_kernel(
                 bank[:], mixed_block, w[k][kb][:, columns_of(half)], start=False, stop=k == K - 1 and kb == NB - 1
             )
 
-        turn_columns(0)
-        r_banks = [[open_gate(R, b, half, state_bf) for half in range(HALVES)] for b in range(B)]
-        for kb in range(NB):
-            if kb + 1 < NB:
-                turn_columns(kb + 1)
-            for b in range(B):
-                for half in range(HALVES):
-                    diffuse(r_banks[b][half], mixed[b][kb][:, 0, R * P : (R + 1) * P], 1, kb, half)
+        places = [(b, half) for b in range(B) for half in range(HALVES)]
+        r_banks = {place: banks.tile([P, HALF], F32, name="r_bank", tag="bank") for place in places}
+        n = 0
+        for z in range(2):
+            for b, half in places:
+                turn(n)
+                n += 1
+                direct(r_banks[(b, half)], R, b, half, z, state_bf)
+        for k in range(1, K):
+            for kb in range(NB):
+                for b, half in places:
+                    if n < TURNS:
+                        turn(n)
+                    n += 1
+                    diffuse(r_banks[(b, half)], mixed[b][kb][:, k - 1, R * P : (R + 1) * P], k, kb, half)
         reset_rows = [held.tile([P, NODES], BF16, name=f"reset_rows{b}") for b in range(B)]
-        for b in range(B):
-            for half in range(HALVES):
-                for kb in range(NB):
-                    diffuse(r_banks[b][half], mixed[b][kb][:, 1, R * P : (R + 1) * P], 2, kb, half)
-                r = work.tile([P, HALF], F32, name="r")
-                nc.scalar.activation(r[:], r_banks[b][half][:], SIGMOID, bias=b_r[:, 0:1])
-                nc.vector.tensor_tensor(
-                    reset_rows[b][:, columns_of(half)], r[:], state_rows[b][:, columns_of(half)], MULT
-                )
+        for b, half in places:
+            r = work.tile([P, HALF], F32, name="r")
+            nc.scalar.activation(r[:], r_banks[(b, half)][:], SIGMOID, bias=b_r[:, 0:1])
+            nc.vector.tensor_tensor(reset_rows[b][:, columns_of(half)], r[:], state_rows[b][:, columns_of(half)], MULT)
 
         mixed_c, keep, rest = [], [], []
         for b in range(B):
+            kept = held.tile([P, NODES], F32, name=f"keep{b}")
+            left = held.tile([P, NODES], F32, name=f"rest{b}")
+            for half in range(HALVES):
+                bank = open_gate(U, b, half, state_bf)
+                for k in range(1, K):
+                    for kb in range(NB):
+                        diffuse(bank, mixed[b][kb][:, k - 1, U * P : (U + 1) * P], k, kb, half)
+                u = work.tile([P, HALF], F32, name="u")
+                nc.scalar.activation(u[:], bank[:], SIGMOID, bias=b_u[:, 0:1])
+                nc.vector.tensor_tensor(kept[:, columns_of(half)], u[:], state_rows[b][:, columns_of(half)], MULT)
+                nc.vector.tensor_scalar(left[:, columns_of(half)], u[:], -1.0, 1.0, MULT, ADD)
+            keep.append(kept)
+            rest.append(left)
+
             pairs = []
             for pair in range(NB // 2):
                 bank = banks.tile([P, 2, 2, P], F32, name="mix_c_bank", tag="bank")
@@ -179,20 +208,6 @@ def tile_dcrnncell_b_kernel(
                 empty(rounded, bank, pair)
                 pairs.append(rounded)
             mixed_c.append(pairs)
-
-            kept = held.tile([P, NODES], F32, name=f"keep{b}")
-            left = held.tile([P, NODES], F32, name=f"rest{b}")
-            for half in range(HALVES):
-                bank = open_gate(U, b, half, state_bf)
-                for k in range(1, K):
-                    for kb in range(NB):
-                        diffuse(bank, mixed[b][kb][:, k - 1, U * P : (U + 1) * P], k, kb, half)
-                u = work.tile([P, HALF], F32, name="u")
-                nc.scalar.activation(u[:], bank[:], SIGMOID, bias=b_u[:, 0:1])
-                nc.vector.tensor_tensor(kept[:, columns_of(half)], u[:], state_rows[b][:, columns_of(half)], MULT)
-                nc.vector.tensor_scalar(left[:, columns_of(half)], u[:], -1.0, 1.0, MULT, ADD)
-            keep.append(kept)
-            rest.append(left)
 
         for b in range(B):
             fresh = held.tile([P, NODES], F32, name=f"fresh{b}")

@@ -36,15 +36,14 @@ def tile_dcrnncell_b_kernel(
         theta_in = held.tile([P, K, GATES * P], BF16, name="theta_in")
         theta_hid = held.tile([P, K, GATES * P], BF16, name="theta_hid")
 
-        def load_theta(theta, g):
+        def load_theta(held_rows, theta, g, z):
             blocks = theta.rearrange("(k z p) h -> z p k h", z=2, p=P)
-            nc.sync.dma_start(theta_in[:, :, g * P : (g + 1) * P], blocks[0, :, :, :])
-            nc.sync.dma_start(theta_hid[:, :, g * P : (g + 1) * P], blocks[1, :, :, :])
+            nc.sync.dma_start(held_rows[:, :, g * P : (g + 1) * P], blocks[z, :, :, :])
 
         def load_bias(bias, name):
             shift = held.tile([P, 1], F32, name=f"bias_{name}")
             with nc.allow_non_contiguous_dma(reason="one float32 of the bias to each partition"):
-                nc.scalar.dma_start(shift[:], bias)
+                nc.sync.dma_start(shift[:], bias)
             return shift
 
         def load_rows(source, columns, dtype, name, block):
@@ -52,24 +51,28 @@ def tile_dcrnncell_b_kernel(
             nc.sync.dma_start(rows[:], source[block * P : (block + 1) * P, :])
             return rows
 
-        load_theta(theta_r, R)
-        load_theta(theta_u, U)
-        x_rows, state_rows = [], []
-        for b in range(B):
+        load_theta(theta_in, theta_r, R, 0)
+        load_theta(theta_in, theta_u, U, 0)
+        x_rows = [load_rows(x, NODES, BF16, "x", 0)]
+        state_rows = [load_rows(state, NODES, F32, "state", 0)]
+        load_theta(theta_hid, theta_r, R, 1)
+        load_theta(theta_hid, theta_u, U, 1)
+        for b in range(1, B):
             x_rows.append(load_rows(x, NODES, BF16, "x", b))
             state_rows.append(load_rows(state, NODES, F32, "state", b))
-        load_theta(theta_c, C)
         adj_rows = [load_rows(adj, NODES, F32, "adj", kb) for kb in range(NB)]
+        load_theta(theta_in, theta_c, C, 0)
+        load_theta(theta_hid, theta_c, C, 1)
+        b_r, b_u, b_c = load_bias(bias_r, "r"), load_bias(bias_u, "u"), load_bias(bias_c, "c")
         offsets = held.tile([P, NODES // 16], U16, name="offsets")
         nc.sync.dma_start(offsets[:], offs)
         window = [load_rows(base, STORE, F32, "window", b) for b in range(B)]
-        b_r, b_u, b_c = load_bias(bias_r, "r"), load_bias(bias_u, "u"), load_bias(bias_c, "c")
 
         ident_f32 = held.tile([P, P], F32, name="ident_f32")
         make_identity(nc, ident_f32[:])
 
         def empty(rounded, bank, turn):
-            if turn % 2 == 0:
+            if turn % 3 < 2:
                 nc.scalar.copy(rounded[:], bank[:])
             else:
                 nc.vector.tensor_copy(rounded[:], bank[:])
@@ -110,7 +113,7 @@ def tile_dcrnncell_b_kernel(
             nc.vector.reduce_sum(total[:], adj_rows[kb][:], axis=mybir.AxisListType.X)
             share = stats.tile([P, 1], F32, name="row_share")
             nc.vector.reciprocal(share[:], total[:])
-            nc.scalar.activation(w1[kb][:], adj_rows[kb][:], COPY, scale=share[:, 0:1])
+            nc.gpsimd.tensor_scalar(w1[kb][:], adj_rows[kb][:], share[:, 0:1], 0.0, MULT, ADD)
 
         making = {}
 

@@ -12,6 +12,8 @@ HALVES = NODES // HALF
 R, U, C = 0, 1, 2
 GATES = 3
 TURNS = NB * NB
+RANGES = [slice(0, HALF), slice(HALF, NODES)]
+LAST_RANGES = [slice(0, 512), slice(512, 768), slice(768, 896), slice(896, 1024)]
 
 FLOPS = 2 * 3 * B * P * NODES * NODES * 2 + 2 * 3 * B * (2 * K * P) * P * NODES
 
@@ -140,22 +142,18 @@ def tile_dcrnncell_b_kernel(
                 nc.vector.reciprocal(share[:], total[:])
                 nc.vector.tensor_scalar_mul(w2[kb][:], making["rows"][:], share[:, 0:1])
 
-        def direct(bank, g, b, half, z, hidden):
+        def direct(bank, g, b, columns, z, hidden):
             weights, rows = ((theta_in, x_rows), (theta_hid, hidden))[z]
-            nc.tensor.matmul(
-                bank[:], weights[:, 0, g * P : (g + 1) * P], rows[b][:, columns_of(half)], start=z == 0, stop=False
-            )
+            nc.tensor.matmul(bank[:], weights[:, 0, g * P : (g + 1) * P], rows[b][:, columns], start=z == 0, stop=False)
 
-        def open_gate(g, b, half, hidden):
-            bank = banks.tile([P, HALF], F32, name="gate_bank", tag="bank")
+        def open_gate(g, b, columns, hidden):
+            bank = banks.tile([P, columns.stop - columns.start], F32, name="gate_bank", tag="bank")
             for z in range(2):
-                direct(bank, g, b, half, z, hidden)
+                direct(bank, g, b, columns, z, hidden)
             return bank
 
-        def diffuse(bank, mixed_block, k, kb, half):
-            nc.tensor.matmul(
-                bank[:], mixed_block, w[k][kb][:, columns_of(half)], start=False, stop=k == K - 1 and kb == NB - 1
-            )
+        def diffuse(bank, mixed_block, k, kb, columns):
+            nc.tensor.matmul(bank[:], mixed_block, w[k][kb][:, columns], start=False, stop=k == K - 1 and kb == NB - 1)
 
         places = [(b, half) for b in range(B) for half in range(HALVES)]
         r_banks = {place: banks.tile([P, HALF], F32, name="r_bank", tag="bank") for place in places}
@@ -164,14 +162,14 @@ def tile_dcrnncell_b_kernel(
             for b, half in places:
                 turn(n)
                 n += 1
-                direct(r_banks[(b, half)], R, b, half, z, state_bf)
+                direct(r_banks[(b, half)], R, b, columns_of(half), z, state_bf)
         for k in range(1, K):
             for kb in range(NB):
                 for b, half in places:
                     if n < TURNS:
                         turn(n)
                     n += 1
-                    diffuse(r_banks[(b, half)], mixed[b][kb][:, k - 1, R * P : (R + 1) * P], k, kb, half)
+                    diffuse(r_banks[(b, half)], mixed[b][kb][:, k - 1, R * P : (R + 1) * P], k, kb, columns_of(half))
         reset_rows = [held.tile([P, NODES], BF16, name=f"reset_rows{b}") for b in range(B)]
         for b, half in places:
             r = work.tile([P, HALF], F32, name="r")
@@ -183,10 +181,10 @@ def tile_dcrnncell_b_kernel(
             kept = held.tile([P, NODES], F32, name=f"keep{b}")
             left = held.tile([P, NODES], F32, name=f"rest{b}")
             for half in range(HALVES):
-                bank = open_gate(U, b, half, state_bf)
+                bank = open_gate(U, b, columns_of(half), state_bf)
                 for k in range(1, K):
                     for kb in range(NB):
-                        diffuse(bank, mixed[b][kb][:, k - 1, U * P : (U + 1) * P], k, kb, half)
+                        diffuse(bank, mixed[b][kb][:, k - 1, U * P : (U + 1) * P], k, kb, columns_of(half))
                 u = work.tile([P, HALF], F32, name="u")
                 nc.scalar.activation(u[:], bank[:], SIGMOID, bias=b_u[:, 0:1])
                 nc.vector.tensor_tensor(kept[:, columns_of(half)], u[:], state_rows[b][:, columns_of(half)], MULT)
@@ -214,13 +212,13 @@ def tile_dcrnncell_b_kernel(
 
         for b in range(B):
             fresh = held.tile([P, NODES], F32, name=f"fresh{b}")
-            for half in range(HALVES):
-                bank = open_gate(C, b, half, reset_rows)
+            for columns in LAST_RANGES if b == B - 1 else RANGES:
+                bank = open_gate(C, b, columns, reset_rows)
                 for k in range(1, K):
                     for kb in range(NB):
-                        diffuse(bank, mixed_c[b][kb // 2][:, kb % 2, k - 1, :], k, kb, half)
-                cand = work.tile([P, HALF], F32, name="cand")
+                        diffuse(bank, mixed_c[b][kb // 2][:, kb % 2, k - 1, :], k, kb, columns)
+                cand = work.tile([P, columns.stop - columns.start], F32, name="cand")
                 nc.scalar.activation(cand[:], bank[:], TANH, bias=b_c[:, 0:1])
-                nc.vector.tensor_tensor(fresh[:, columns_of(half)], rest[b][:, columns_of(half)], cand[:], MULT)
+                nc.vector.tensor_tensor(fresh[:, columns], rest[b][:, columns], cand[:], MULT)
             nc.vector.tensor_tensor(window[b][:].indirect(offsets[:]), keep[b][:], fresh[:], ADD)
             nc.sync.dma_start(out[b * P : (b + 1) * P, :], window[b][:])

@@ -180,15 +180,16 @@ def tile_dcrnncell_b_kernel(
         for b in range(B):
             kept = held.tile([P, NODES], F32, name=f"keep{b}")
             left = held.tile([P, NODES], F32, name=f"rest{b}")
-            for half in range(HALVES):
-                bank = open_gate(U, b, columns_of(half), state_bf)
-                for k in range(1, K):
-                    for kb in range(NB):
-                        diffuse(bank, mixed[b][kb][:, k - 1, U * P : (U + 1) * P], k, kb, columns_of(half))
+            u_banks = [open_gate(U, b, columns, state_bf) for columns in RANGES]
+            for k in range(1, K):
+                for kb in range(NB):
+                    for bank, columns in zip(u_banks, RANGES):
+                        diffuse(bank, mixed[b][kb][:, k - 1, U * P : (U + 1) * P], k, kb, columns)
+            for bank, columns in zip(u_banks, RANGES):
                 u = work.tile([P, HALF], F32, name="u")
                 nc.scalar.activation(u[:], bank[:], SIGMOID, bias=b_u[:, 0:1])
-                nc.vector.tensor_tensor(kept[:, columns_of(half)], u[:], state_rows[b][:, columns_of(half)], MULT)
-                nc.vector.tensor_scalar(left[:, columns_of(half)], u[:], -1.0, 1.0, MULT, ADD)
+                nc.vector.tensor_tensor(kept[:, columns], u[:], state_rows[b][:, columns], MULT)
+                nc.vector.tensor_scalar(left[:, columns], u[:], -1.0, 1.0, MULT, ADD)
             keep.append(kept)
             rest.append(left)
 
@@ -212,13 +213,15 @@ def tile_dcrnncell_b_kernel(
 
         for b in range(B):
             fresh = held.tile([P, NODES], F32, name=f"fresh{b}")
-            for columns in LAST_RANGES if b == B - 1 else RANGES:
-                bank = open_gate(C, b, columns, reset_rows)
+            for together in [[columns] for columns in LAST_RANGES] if b == B - 1 else [RANGES]:
+                c_banks = [open_gate(C, b, columns, reset_rows) for columns in together]
                 for k in range(1, K):
                     for kb in range(NB):
-                        diffuse(bank, mixed_c[b][kb // 2][:, kb % 2, k - 1, :], k, kb, columns)
-                cand = work.tile([P, columns.stop - columns.start], F32, name="cand")
-                nc.scalar.activation(cand[:], bank[:], TANH, bias=b_c[:, 0:1])
-                nc.vector.tensor_tensor(fresh[:, columns], rest[b][:, columns], cand[:], MULT)
+                        for bank, columns in zip(c_banks, together):
+                            diffuse(bank, mixed_c[b][kb // 2][:, kb % 2, k - 1, :], k, kb, columns)
+                for bank, columns in zip(c_banks, together):
+                    cand = work.tile([P, columns.stop - columns.start], F32, name="cand")
+                    nc.scalar.activation(cand[:], bank[:], TANH, bias=b_c[:, 0:1])
+                    nc.vector.tensor_tensor(fresh[:, columns], rest[b][:, columns], cand[:], MULT)
             nc.vector.tensor_tensor(window[b][:].indirect(offsets[:]), keep[b][:], fresh[:], ADD)
             nc.sync.dma_start(out[b * P : (b + 1) * P, :], window[b][:])

@@ -157,12 +157,10 @@ def tile_dcrnncell_b_kernel(
 
         places = [(b, half) for b in range(B) for half in range(HALVES)]
         r_banks = {place: banks.tile([P, HALF], F32, name="r_bank", tag="bank") for place in places}
-        n = 0
         for z in range(2):
             for b, half in places:
-                turn(n)
-                n += 1
                 direct(r_banks[(b, half)], R, b, columns_of(half), z, state_bf)
+        n = 0
         for k in range(1, K):
             for kb in range(NB):
                 for b, half in places:

@@ -38,9 +38,9 @@ def tile_dcrnncell_b_kernel(
         theta_in = held.tile([P, K, GATES * P], BF16, name="theta_in")
         theta_hid = held.tile([P, K, GATES * P], BF16, name="theta_hid")
 
-        def load_theta(held_rows, theta, g, z):
+        def load_theta(held_rows, theta, g, z, steps=slice(0, K)):
             blocks = theta.rearrange("(k z p) h -> z p k h", z=2, p=P)
-            nc.sync.dma_start(held_rows[:, :, g * P : (g + 1) * P], blocks[z, :, :, :])
+            nc.sync.dma_start(held_rows[:, steps, g * P : (g + 1) * P], blocks[z, :, steps, :])
 
         def load_bias(bias, name):
             shift = held.tile([P, 1], F32, name=f"bias_{name}")
@@ -53,9 +53,12 @@ def tile_dcrnncell_b_kernel(
             nc.sync.dma_start(rows[:], source[block * P : (block + 1) * P, :])
             return rows
 
-        load_theta(theta_in, theta_r, R, 0)
+        load_theta(theta_in, theta_r, R, 0, slice(0, 1))
+        x_rows = [held.tile([P, NODES], BF16, name="x0")]
+        for columns in RANGES:
+            nc.sync.dma_start(x_rows[0][:, columns], x[0:P, columns])
+        load_theta(theta_in, theta_r, R, 0, slice(1, K))
         load_theta(theta_in, theta_u, U, 0)
-        x_rows = [load_rows(x, NODES, BF16, "x", 0)]
         state_rows = [load_rows(state, NODES, F32, "state", 0)]
         load_theta(theta_hid, theta_r, R, 1)
         load_theta(theta_hid, theta_u, U, 1)
@@ -84,6 +87,20 @@ def tile_dcrnncell_b_kernel(
 
         def nodes_of(kb):
             return slice(kb * P, (kb + 1) * P)
+
+        def direct(bank, g, b, columns, z, hidden):
+            weights, rows = ((theta_in, x_rows), (theta_hid, hidden))[z]
+            nc.tensor.matmul(bank[:], weights[:, 0, g * P : (g + 1) * P], rows[b][:, columns], start=z == 0, stop=False)
+
+        places = [(b, half) for b in range(B) for half in range(HALVES)]
+        r_banks = {}
+
+        def open_r(b):
+            for half in range(HALVES):
+                r_banks[(b, half)] = banks.tile([P, HALF], F32, name="r_bank", tag="bank")
+                direct(r_banks[(b, half)], R, b, columns_of(half), 0, x_rows)
+
+        open_r(0)
 
         state_bf = []
         for b in range(B):
@@ -142,10 +159,6 @@ def tile_dcrnncell_b_kernel(
                 nc.vector.reciprocal(share[:], total[:])
                 nc.vector.tensor_scalar_mul(w2[kb][:], making["rows"][:], share[:, 0:1])
 
-        def direct(bank, g, b, columns, z, hidden):
-            weights, rows = ((theta_in, x_rows), (theta_hid, hidden))[z]
-            nc.tensor.matmul(bank[:], weights[:, 0, g * P : (g + 1) * P], rows[b][:, columns], start=z == 0, stop=False)
-
         def open_gate(g, b, columns, hidden):
             bank = banks.tile([P, columns.stop - columns.start], F32, name="gate_bank", tag="bank")
             for z in range(2):
@@ -155,11 +168,10 @@ def tile_dcrnncell_b_kernel(
         def diffuse(bank, mixed_block, k, kb, columns):
             nc.tensor.matmul(bank[:], mixed_block, w[k][kb][:, columns], start=False, stop=k == K - 1 and kb == NB - 1)
 
-        places = [(b, half) for b in range(B) for half in range(HALVES)]
-        r_banks = {place: banks.tile([P, HALF], F32, name="r_bank", tag="bank") for place in places}
-        for z in range(2):
-            for b, half in places:
-                direct(r_banks[(b, half)], R, b, columns_of(half), z, state_bf)
+        for b in range(1, B):
+            open_r(b)
+        for b, half in places:
+            direct(r_banks[(b, half)], R, b, columns_of(half), 1, state_bf)
         n = 0
         for k in range(1, K):
             for kb in range(NB):

@@ -13,7 +13,7 @@ R, U, C = 0, 1, 2
 GATES = 3
 TURNS = NB * NB
 RANGES = [slice(0, HALF), slice(HALF, NODES)]
-LAST_RANGES = [slice(0, 512), slice(512, 768), slice(768, 896), slice(896, 1024)]
+LAST_RANGES = [slice(0, 512), slice(512, 832), slice(832, 960), slice(960, 1024)]
 
 FLOPS = 2 * 3 * B * P * NODES * NODES * 2 + 2 * 3 * B * (2 * K * P) * P * NODES
 
@@ -53,15 +53,18 @@ def tile_dcrnncell_b_kernel(
             nc.sync.dma_start(rows[:], source[block * P : (block + 1) * P, :])
             return rows
 
-        load_theta(theta_in, theta_r, R, 0, slice(0, 1))
         x_rows = [held.tile([P, NODES], BF16, name="x0")]
+        state_rows = [held.tile([P, NODES], F32, name="state0")]
+        first, second = RANGES
+        load_theta(theta_in, theta_r, R, 0, slice(0, 1))
         for columns in RANGES:
             nc.sync.dma_start(x_rows[0][:, columns], x[0:P, columns])
         load_theta(theta_in, theta_r, R, 0, slice(1, K))
         load_theta(theta_in, theta_u, U, 0)
-        state_rows = [load_rows(state, NODES, F32, "state", 0)]
+        nc.sync.dma_start(state_rows[0][:, first], state[0:P, first])
         load_theta(theta_hid, theta_r, R, 1)
         load_theta(theta_hid, theta_u, U, 1)
+        nc.sync.dma_start(state_rows[0][:, second], state[0:P, second])
         for b in range(1, B):
             x_rows.append(load_rows(x, NODES, BF16, "x", b))
             state_rows.append(load_rows(state, NODES, F32, "state", b))
@@ -105,7 +108,8 @@ def tile_dcrnncell_b_kernel(
         state_bf = []
         for b in range(B):
             rounded_state = held.tile([P, NODES], BF16, name=f"state_bf{b}")
-            nc.vector.tensor_copy(rounded_state[:], state_rows[b][:])
+            for columns in RANGES:
+                nc.vector.tensor_copy(rounded_state[:, columns], state_rows[b][:, columns])
             state_bf.append(rounded_state)
 
         mixed = []

@@ -190,10 +190,9 @@ def tile_dcrnncell_b_kernel(
             nc.scalar.activation(r[:], r_banks[(b, half)][:], SIGMOID, bias=b_r[:, 0:1])
             nc.vector.tensor_tensor(reset_rows[b][:, columns_of(half)], r[:], state_rows[b][:, columns_of(half)], MULT)
 
-        mixed_c, keep, rest = [], [], []
         for b in range(B):
-            kept = held.tile([P, NODES], F32, name=f"keep{b}")
-            left = held.tile([P, NODES], F32, name=f"rest{b}")
+            keep = held.tile([P, NODES], F32, name=f"keep{b}")
+            rest = held.tile([P, NODES], F32, name=f"rest{b}")
             u_banks = [open_gate(U, b, columns, state_bf) for columns in RANGES]
             for k in range(1, K):
                 for kb in range(NB):
@@ -202,12 +201,10 @@ def tile_dcrnncell_b_kernel(
             for bank, columns in zip(u_banks, RANGES):
                 u = work.tile([P, HALF], F32, name="u")
                 nc.scalar.activation(u[:], bank[:], SIGMOID, bias=b_u[:, 0:1])
-                nc.vector.tensor_tensor(kept[:, columns], u[:], state_rows[b][:, columns], MULT)
-                nc.vector.tensor_scalar(left[:, columns], u[:], -1.0, 1.0, MULT, ADD)
-            keep.append(kept)
-            rest.append(left)
+                nc.vector.tensor_tensor(keep[:, columns], u[:], state_rows[b][:, columns], MULT)
+                nc.vector.tensor_scalar(rest[:, columns], u[:], -1.0, 1.0, MULT, ADD)
 
-            pairs = []
+            mixed_c = []
             for pair in range(NB // 2):
                 bank = banks.tile([P, 2, 2, P], F32, name="mix_c_bank", tag="bank")
                 for j in range(2):
@@ -222,20 +219,18 @@ def tile_dcrnncell_b_kernel(
                     )
                 rounded = held.tile([P, 2, 2, P], BF16, name=f"mixed_c{b}_{pair}")
                 empty(rounded, bank, pair)
-                pairs.append(rounded)
-            mixed_c.append(pairs)
+                mixed_c.append(rounded)
 
-        for b in range(B):
             fresh = held.tile([P, NODES], F32, name=f"fresh{b}")
             for together in [[columns] for columns in LAST_RANGES] if b == B - 1 else [RANGES]:
                 c_banks = [open_gate(C, b, columns, reset_rows) for columns in together]
                 for k in range(1, K):
                     for kb in range(NB):
                         for bank, columns in zip(c_banks, together):
-                            diffuse(bank, mixed_c[b][kb // 2][:, kb % 2, k - 1, :], k, kb, columns)
+                            diffuse(bank, mixed_c[kb // 2][:, kb % 2, k - 1, :], k, kb, columns)
                 for bank, columns in zip(c_banks, together):
                     cand = work.tile([P, columns.stop - columns.start], F32, name="cand")
                     nc.scalar.activation(cand[:], bank[:], TANH, bias=b_c[:, 0:1])
-                    nc.vector.tensor_tensor(fresh[:, columns], rest[b][:, columns], cand[:], MULT)
-            nc.vector.tensor_tensor(window[b][:].indirect(offsets[:]), keep[b][:], fresh[:], ADD)
+                    nc.vector.tensor_tensor(fresh[:, columns], rest[:, columns], cand[:], MULT)
+            nc.vector.tensor_tensor(window[b][:].indirect(offsets[:]), keep[:], fresh[:], ADD)
             nc.sync.dma_start(out[b * P : (b + 1) * P, :], window[b][:])

import concourse.mybir as mybir
from concourse.masks import make_identity

P = 128
B = 3
K = 3
NODES = 1024
STORE = 2048
NB = NODES // P
HALF = 512
HALVES = NODES // HALF
R, U, C = 0, 1, 2
GATES = 3
TURNS = NB * NB
RANGES = [slice(0, HALF), slice(HALF, NODES)]
LAST_RANGES = [slice(0, 512), slice(512, 832), slice(832, 960), slice(960, 1024)]

FLOPS = 2 * 3 * B * P * NODES * NODES * 2 + 2 * 3 * B * (2 * K * P) * P * NODES

BF16, F32, U16 = mybir.dt.bfloat16, mybir.dt.float32, mybir.dt.uint16
MULT, ADD = mybir.AluOpType.mult, mybir.AluOpType.add
COPY = mybir.ActivationFunctionType.Copy
SIGMOID = mybir.ActivationFunctionType.Sigmoid
TANH = mybir.ActivationFunctionType.Tanh


def tile_dcrnncell_b_kernel(
    tc, x, state, adj, theta_r, theta_u, theta_c, bias_r, bias_u, bias_c, base, offs, out
):
    nc = tc.nc
    with (
        tc.tile_pool(name="held", bufs=1) as held,
        tc.tile_pool(name="staging", bufs=2) as staging,
        tc.tile_pool(name="stats", bufs=4) as stats,
        tc.tile_pool(name="work", bufs=3) as work,
        tc.psum_pool(name="banks", bufs=8) as banks,
    ):
        theta_in = held.tile([P, K, GATES * P], BF16, name="theta_in")
        theta_hid = held.tile([P, K, GATES * P], BF16, name="theta_hid")

        def load_theta(held_rows, theta, g, z, steps=slice(0, K)):
            blocks = theta.rearrange("(k z p) h -> z p k h", z=2, p=P)
            nc.sync.dma_start(held_rows[:, steps, g * P : (g + 1) * P], blocks[z, :, steps, :])

        def load_bias(bias, name):
            shift = held.tile([P, 1], F32, name=f"bias_{name}")
            with nc.allow_non_contiguous_dma(reason="one float32 of the bias to each partition"):
                nc.sync.dma_start(shift[:], bias)
            return shift

        def load_rows(source, columns, dtype, name, block):
            rows = held.tile([P, columns], dtype, name=f"{name}{block}")
            nc.sync.dma_start(rows[:], source[block * P : (block + 1) * P, :])
            return rows

        x_rows = [held.tile([P, NODES], BF16, name="x0")]
        state_rows = [held.tile([P, NODES], F32, name="state0")]
        first, second = RANGES
        load_theta(theta_in, theta_r, R, 0, slice(0, 1))
        for columns in RANGES:
            nc.sync.dma_start(x_rows[0][:, columns], x[0:P, columns])
        load_theta(theta_in, theta_r, R, 0, slice(1, K))
        load_theta(theta_in, theta_u, U, 0)
        nc.sync.dma_start(state_rows[0][:, first], state[0:P, first])
        load_theta(theta_hid, theta_r, R, 1)
        load_theta(theta_hid, theta_u, U, 1)
        nc.sync.dma_start(state_rows[0][:, second], state[0:P, second])
        for b in range(1, B):
            x_rows.append(load_rows(x, NODES, BF16, "x", b))
            state_rows.append(load_rows(state, NODES, F32, "state", b))
        adj_rows = [load_rows(adj, NODES, F32, "adj", kb) for kb in range(NB)]
        load_theta(theta_in, theta_c, C, 0)
        load_theta(theta_hid, theta_c, C, 1)
        b_r, b_u, b_c = load_bias(bias_r, "r"), load_bias(bias_u, "u"), load_bias(bias_c, "c")
        offsets = held.tile([P, NODES // 16], U16, name="offsets")
        nc.sync.dma_start(offsets[:], offs)
        window = [load_rows(base, STORE, F32, "window", b) for b in range(B)]

        ident_f32 = held.tile([P, P], F32, name="ident_f32")
        make_identity(nc, ident_f32[:])

        def empty(rounded, bank, turn):
            if turn % 3 < 2:
                nc.scalar.copy(rounded[:], bank[:])
            else:
                nc.vector.tensor_copy(rounded[:], bank[:])

        def columns_of(half):
            return slice(half * HALF, (half + 1) * HALF)

        def nodes_of(kb):
            return slice(kb * P, (kb + 1) * P)

        def direct(bank, g, b, columns, z, hidden):
            weights, rows = ((theta_in, x_rows), (theta_hid, hidden))[z]
            nc.tensor.matmul(bank[:], weights[:, 0, g * P : (g + 1) * P], rows[b][:, columns], start=z == 0, stop=False)

        places = [(b, half) for b in range(B) for half in range(HALVES)]
        r_banks = {}

        def open_r(b):
            for half in range(HALVES):
                r_banks[(b, half)] = banks.tile([P, HALF], F32, name="r_bank", tag="bank")
                direct(r_banks[(b, half)], R, b, columns_of(half), 0, x_rows)

        open_r(0)

        state_bf = []
        for b in range(B):
            rounded_state = held.tile([P, NODES], BF16, name=f"state_bf{b}")
            for columns in RANGES:
                nc.vector.tensor_copy(rounded_state[:, columns], state_rows[b][:, columns])
            state_bf.append(rounded_state)

        mixed = []
        for b in range(B):
            blocks = []
            for kb in range(NB):
                bank = banks.tile([P, 2, 2 * P], F32, name="mix_bank", tag="bank")
                nc.tensor.matmul(
                    bank[:], x_rows[b][:, nodes_of(kb)], theta_in[:, 1:K, 0 : 2 * P], start=True, stop=False
                )
                nc.tensor.matmul(
                    bank[:], state_bf[b][:, nodes_of(kb)], theta_hid[:, 1:K, 0 : 2 * P], start=False, stop=True
                )
                rounded = held.tile([P, 2, 2 * P], BF16, name=f"mixed{b}_{kb}")
                empty(rounded, bank, kb)
                blocks.append(rounded)
            mixed.append(blocks)

        w1 = [held.tile([P, NODES], BF16, name=f"w1_{kb}") for kb in range(NB)]
        w2 = [held.tile([P, NODES], BF16, name=f"w2_{kb}") for kb in range(NB)]
        w = [None, w1, w2]
        for kb in range(NB):
            total = stats.tile([P, 1], F32, name="row_total")
            nc.vector.reduce_sum(total[:], adj_rows[kb][:], axis=mybir.AxisListType.X)
            share = stats.tile([P, 1], F32, name="row_share")
            nc.vector.reciprocal(share[:], total[:])
            nc.gpsimd.tensor_scalar(w1[kb][:], adj_rows[kb][:], share[:, 0:1], 0.0, MULT, ADD)

        making = {}

        def turn(n):
            kb, piece = divmod(n, NB)
            half, j = divmod(piece, HALF // P)
            if piece == 0:
                making["rows"] = staging.tile([P, NODES], F32, name="turned_rows")
                making["parts"] = stats.tile([P, HALVES], F32, name="column_parts")
            if j == 0:
                making["bank"] = banks.tile([P, HALF], F32, name="adj_bank", tag="bank")
            nc.tensor.transpose(making["bank"][:, nodes_of(j)], adj_rows[piece][:, nodes_of(kb)], ident_f32[:])
            if j == HALF // P - 1:
                nc.scalar.activation(
                    making["rows"][:, columns_of(half)],
                    making["bank"][:],
                    COPY,
                    accum_out=making["parts"][:, half : half + 1],
                )
            if piece == NB - 1:
                total = stats.tile([P, 1], F32, name="column_total")
                nc.vector.reduce_sum(total[:], making["parts"][:], axis=mybir.AxisListType.X)
                share = stats.tile([P, 1], F32, name="column_share")
                nc.vector.reciprocal(share[:], total[:])
                nc.vector.tensor_scalar_mul(w2[kb][:], making["rows"][:], share[:, 0:1])

        def open_gate(g, b, columns, hidden):
            bank = banks.tile([P, columns.stop - columns.start], F32, name="gate_bank", tag="bank")
            for z in range(2):
                direct(bank, g, b, columns, z, hidden)
            return bank

        def diffuse(bank, mixed_block, k, kb, columns):
            nc.tensor.matmul(bank[:], mixed_block, w[k][kb][:, columns], start=False, stop=k == K - 1 and kb == NB - 1)

        for b in range(1, B):
            open_r(b)
        for b, half in places:
            direct(r_banks[(b, half)], R, b, columns_of(half), 1, state_bf)
        n = 0
        for k in range(1, K):
            for kb in range(NB):
                for b, half in places:
                    if n < TURNS:
                        turn(n)
                    n += 1
                    diffuse(r_banks[(b, half)], mixed[b][kb][:, k - 1, R * P : (R + 1) * P], k, kb, columns_of(half))
        reset_rows = [held.tile([P, NODES], BF16, name=f"reset_rows{b}") for b in range(B)]
        for b, half in places:
            r = work.tile([P, HALF], F32, name="r")
            nc.scalar.activation(r[:], r_banks[(b, half)][:], SIGMOID, bias=b_r[:, 0:1])
            nc.vector.tensor_tensor(reset_rows[b][:, columns_of(half)], r[:], state_rows[b][:, columns_of(half)], MULT)

        for b in range(B):
            keep = held.tile([P, NODES], F32, name=f"keep{b}")
            rest = held.tile([P, NODES], F32, name=f"rest{b}")
            u_banks = [open_gate(U, b, columns, state_bf) for columns in RANGES]
            for k in range(1, K):
                for kb in range(NB):
                    for bank, columns in zip(u_banks, RANGES):
                        diffuse(bank, mixed[b][kb][:, k - 1, U * P : (U + 1) * P], k, kb, columns)
            for bank, columns in zip(u_banks, RANGES):
                u = work.tile([P, HALF], F32, name="u")
                nc.scalar.activation(u[:], bank[:], SIGMOID, bias=b_u[:, 0:1])
                nc.vector.tensor_tensor(keep[:, columns], u[:], state_rows[b][:, columns], MULT)
                nc.vector.tensor_scalar(rest[:, columns], u[:], -1.0, 1.0, MULT, ADD)

            mixed_c = []
            for pair in range(NB // 2):
                bank = banks.tile([P, 2, 2, P], F32, name="mix_c_bank", tag="bank")
                for j in range(2):
                    nodes = nodes_of(2 * pair + j)
                    nc.tensor.matmul(
                        bank[:, j, :, :], x_rows[b][:, nodes], theta_in[:, 1:K, C * P : (C + 1) * P],
                        start=True, stop=False,
                    )
                    nc.tensor.matmul(
                        bank[:, j, :, :], reset_rows[b][:, nodes], theta_hid[:, 1:K, C * P : (C + 1) * P],
                        start=False, stop=True,
                    )
                rounded = held.tile([P, 2, 2, P], BF16, name=f"mixed_c{b}_{pair}")
                empty(rounded, bank, pair)
                mixed_c.append(rounded)

            fresh = held.tile([P, NODES], F32, name=f"fresh{b}")
            for together in [[columns] for columns in LAST_RANGES] if b == B - 1 else [RANGES]:
                c_banks = [open_gate(C, b, columns, reset_rows) for columns in together]
                for k in range(1, K):
                    for kb in range(NB):
                        for bank, columns in zip(c_banks, together):
                            diffuse(bank, mixed_c[kb // 2][:, kb % 2, k - 1, :], k, kb, columns)
                for bank, columns in zip(c_banks, together):
                    cand = work.tile([P, columns.stop - columns.start], F32, name="cand")
                    nc.scalar.activation(cand[:], bank[:], TANH, bias=b_c[:, 0:1])
                    nc.vector.tensor_tensor(fresh[:, columns], rest[:, columns], cand[:], MULT)
            nc.vector.tensor_tensor(window[b][:].indirect(offsets[:]), keep[:], fresh[:], ADD)
            nc.sync.dma_start(out[b * P : (b + 1) * P, :], window[b][:])
